import numpy as np
import ml_dtypes

BF16 = ml_dtypes.bfloat16


def bf(x):
    return np.asarray(x, np.float32).astype(BF16)


def f32(x):
    return np.asarray(x, np.float32)


def f64(x):
    return np.asarray(x).astype(np.float64)


def striped(idx):
    return np.tile(idx.reshape(-1, 16).T, (8, 1))


V, D, M, K, N = 4096, 128, 256, 128, 1024


def sigmoid(v):
    return 1.0 / (1.0 + np.exp(-v))


def setup_inputs():
    return {"table": bf(np.random.standard_normal((D, V))), "wv": bf(np.random.standard_normal((D, M)) / np.sqrt(D)), "bv": f32(0.3 * np.random.standard_normal((M, 1))), "fc_w": bf(np.random.standard_normal((M, K)) / np.sqrt(0.5 * M)), "fc_b": f32(0.3 * np.random.standard_normal((K, 1))), "offs": striped(np.random.permutation(np.tile(np.arange(V), 2))[:N])}


def reference(table, wv, bv, fc_w, fc_b, offs):
    idx = offs[:16].T.reshape(-1)
    h = np.maximum(f64(wv).T @ f64(table)[:, idx] + f64(bv), 0.0)
    return sigmoid(f64(fc_w).T @ h + f64(fc_b))

@@ -1,0 +1,57 @@
+import concourse.mybir as mybir
+
+P = 128
+V = 4096
+HALVES = 2
+N = 1024
+PIECE = 512
+FLOPS = 2 * P * (HALVES * P) * N + 2 * (HALVES * P) * P * N
+
+BF16, F32, U16 = mybir.dt.bfloat16, mybir.dt.float32, mybir.dt.uint16
+ADD, MAX = mybir.AluOpType.add, mybir.AluOpType.max
+RELU, SIGMOID = mybir.ActivationFunctionType.Relu, mybir.ActivationFunctionType.Sigmoid
+
+
+def tile_discriminator_kernel(tc, table, wv, bv, fc_w, fc_b, offs, out):
+    nc = tc.nc
+    with (
+        tc.tile_pool(name="held", bufs=1) as held,
+        tc.tile_pool(name="work", bufs=2) as work,
+        tc.psum_pool(name="psum", bufs=2) as psum,
+    ):
+        offsets = held.tile([P, N // 16], U16, name="offsets")
+        nc.sync.dma_start(offsets[:], offs)
+
+        words = held.tile([P, V], BF16, name="words")
+        nc.sync.dma_start(words[:], table)
+
+        wv_sb = held.tile([P, HALVES * P], BF16, name="wv_sb")
+        nc.scalar.dma_start(wv_sb[:], wv)
+        fcw_sb = held.tile([P, HALVES, P], BF16, name="fcw_sb")
+        nc.scalar.dma_start(fcw_sb[:], fc_w.rearrange("(h p) c -> p h c", p=P))
+        bv_sb = [held.tile([P, 1], F32, name=f"bv_sb{h}") for h in range(HALVES)]
+        for h in range(HALVES):
+            nc.gpsimd.dma_start(bv_sb[h][:], bv[h * P : (h + 1) * P, :])
+        fcb_sb = held.tile([P, 1], F32, name="fcb_sb")
+        nc.gpsimd.dma_start(fcb_sb[:], fc_b)
+
+        for j in range(N // PIECE):
+            piece = offsets[:, j * (PIECE // 16) : (j + 1) * (PIECE // 16)]
+
+            hidden = []
+            for h in range(HALVES):
+                proj = psum.tile([P, PIECE], F32, name=f"proj{h}")
+                nc.tensor.matmul(proj[:], wv_sb[:, h * P : (h + 1) * P], words[:].indirect(piece), start=True, stop=True)
+                hid = work.tile([P, PIECE], BF16, name=f"hid{h}")
+                if h == 0:
+                    nc.vector.tensor_scalar(hid[:], proj[:], bv_sb[h][:], 0.0, ADD, MAX)
+                else:
+                    nc.scalar.activation(hid[:], proj[:], RELU, bias=bv_sb[h][:])
+                hidden.append(hid)
+
+            logit = psum.tile([P, PIECE], F32, name="logit")
+            for h in range(HALVES):
+                nc.tensor.matmul(logit[:], fcw_sb[:, h, :], hidden[h][:], start=(h == 0), stop=(h == HALVES - 1))
+            score = work.tile([P, PIECE], F32, name="score")
+            nc.scalar.activation(score[:], logit[:], SIGMOID, bias=fcb_sb[:])
+            nc.sync.dma_start(out[:, j * PIECE : (j + 1) * PIECE], score[:])

@@ -5,6 +5,8 @@ V = 4096
 HALVES = 2
 N = 1024
 PIECE = 512
+WARM = 8
+LOADS = 4
 FLOPS = 2 * P * (HALVES * P) * N + 2 * (HALVES * P) * P * N
 
 BF16, F32, U16 = mybir.dt.bfloat16, mybir.dt.float32, mybir.dt.uint16
@@ -22,18 +24,31 @@ def tile_discriminator_kernel(tc, table, wv, bv, fc_w, fc_b, offs, out):
         offsets = held.tile([P, N // 16], U16, name="offsets")
         nc.sync.dma_start(offsets[:], offs)
 
-        words = held.tile([P, V], BF16, name="words")
-        nc.sync.dma_start(words[:], table)
-
         wv_sb = held.tile([P, HALVES * P], BF16, name="wv_sb")
         nc.scalar.dma_start(wv_sb[:], wv)
-        fcw_sb = held.tile([P, HALVES, P], BF16, name="fcw_sb")
-        nc.scalar.dma_start(fcw_sb[:], fc_w.rearrange("(h p) c -> p h c", p=P))
         bv_sb = [held.tile([P, 1], F32, name=f"bv_sb{h}") for h in range(HALVES)]
         for h in range(HALVES):
-            nc.gpsimd.dma_start(bv_sb[h][:], bv[h * P : (h + 1) * P, :])
+            nc.scalar.dma_start(bv_sb[h][:], bv[h * P : (h + 1) * P, :])
+
+        words = held.tile([P, V], BF16, name="words")
+        for q in range(LOADS):
+            queue = nc.sync if q % 2 == 0 else nc.scalar
+            queue.dma_start(words[:, q * (V // LOADS) : (q + 1) * (V // LOADS)], table[:, q * (V // LOADS) : (q + 1) * (V // LOADS)])
+
         fcb_sb = held.tile([P, 1], F32, name="fcb_sb")
-        nc.gpsimd.dma_start(fcb_sb[:], fc_b)
+        nc.scalar.dma_start(fcb_sb[:], fc_b)
+        fcw_sb = held.tile([P, HALVES, P], BF16, name="fcw_sb")
+        nc.scalar.dma_start(fcw_sb[:], fc_w.rearrange("(h p) c -> p h c", p=P))
+
+        idle = held.tile([P, PIECE], BF16, name="idle")
+        nc.vector.memset(idle[:], 0.0)
+        spin = psum.tile([P, PIECE], F32, name="spin")
+        for turn in range(WARM):
+            nc.tensor.matmul(spin[:], idle[:, 0:P], idle[:], start=True, stop=True)
+
+        warm = held.tile([P, 1], F32, name="warm")
+        nc.vector.memset(warm[:], 0.0)
+        nc.scalar.activation(warm[:], warm[:], SIGMOID)
 
         for j in range(N // PIECE):
             piece = offsets[:, j * (PIECE // 16) : (j + 1) * (PIECE // 16)]

@@ -4,7 +4,9 @@ P = 128
 V = 4096
 HALVES = 2
 N = 1024
-PIECE = 512
+BANK = 512
+PIECE = BANK
+UNIT = 256
 WARM = 8
 LOADS = 4
 FLOPS = 2 * P * (HALVES * P) * N + 2 * (HALVES * P) * P * N
@@ -18,8 +20,9 @@ def tile_discriminator_kernel(tc, table, wv, bv, fc_w, fc_b, offs, out):
     nc = tc.nc
     with (
         tc.tile_pool(name="held", bufs=1) as held,
-        tc.tile_pool(name="work", bufs=2) as work,
-        tc.psum_pool(name="psum", bufs=2) as psum,
+        tc.tile_pool(name="work", bufs=N // UNIT) as work,
+        tc.psum_pool(name="banks", bufs=1) as banks,
+        tc.psum_pool(name="logits", bufs=3) as logits,
     ):
         offsets = held.tile([P, N // 16], U16, name="offsets")
         nc.sync.dma_start(offsets[:], offs)
@@ -40,9 +43,9 @@ def tile_discriminator_kernel(tc, table, wv, bv, fc_w, fc_b, offs, out):
         fcw_sb = held.tile([P, HALVES, P], BF16, name="fcw_sb")
         nc.scalar.dma_start(fcw_sb[:], fc_w.rearrange("(h p) c -> p h c", p=P))
 
-        idle = held.tile([P, PIECE], BF16, name="idle")
+        idle = held.tile([P, BANK], BF16, name="idle")
         nc.vector.memset(idle[:], 0.0)
-        spin = psum.tile([P, PIECE], F32, name="spin")
+        spin = banks.tile([P, BANK], F32, name="spin")
         for turn in range(WARM):
             nc.tensor.matmul(spin[:], idle[:, 0:P], idle[:], start=True, stop=True)
 
@@ -50,23 +53,27 @@ def tile_discriminator_kernel(tc, table, wv, bv, fc_w, fc_b, offs, out):
         nc.vector.memset(warm[:], 0.0)
         nc.scalar.activation(warm[:], warm[:], SIGMOID)
 
+        proj = [[banks.tile([P, PIECE], F32, name=f"proj{j}{h}") for h in range(HALVES)] for j in range(N // PIECE)]
         for j in range(N // PIECE):
             piece = offsets[:, j * (PIECE // 16) : (j + 1) * (PIECE // 16)]
+            for h in range(HALVES):
+                nc.tensor.matmul(proj[j][h][:], wv_sb[:, h * P : (h + 1) * P], words[:].indirect(piece), start=True, stop=True)
+
+        for u in range(N // UNIT):
+            j, col = divmod(u * UNIT, PIECE)
 
             hidden = []
             for h in range(HALVES):
-                proj = psum.tile([P, PIECE], F32, name=f"proj{h}")
-                nc.tensor.matmul(proj[:], wv_sb[:, h * P : (h + 1) * P], words[:].indirect(piece), start=True, stop=True)
-                hid = work.tile([P, PIECE], BF16, name=f"hid{h}")
-                if h == 0:
-                    nc.vector.tensor_scalar(hid[:], proj[:], bv_sb[h][:], 0.0, ADD, MAX)
+                hid = work.tile([P, UNIT], BF16, name=f"hid{h}")
+                if j == 0 and h == 1:
+                    nc.scalar.activation(hid[:], proj[j][h][:, col : col + UNIT], RELU, bias=bv_sb[h][:])
                 else:
-                    nc.scalar.activation(hid[:], proj[:], RELU, bias=bv_sb[h][:])
+                    nc.vector.tensor_scalar(hid[:], proj[j][h][:, col : col + UNIT], bv_sb[h][:], 0.0, ADD, MAX)
                 hidden.append(hid)
 
-            logit = psum.tile([P, PIECE], F32, name="logit")
+            logit = logits.tile([P, UNIT], F32, name="logit")
             for h in range(HALVES):
                 nc.tensor.matmul(logit[:], fcw_sb[:, h, :], hidden[h][:], start=(h == 0), stop=(h == HALVES - 1))
-            score = work.tile([P, PIECE], F32, name="score")
+            score = work.tile([P, UNIT], F32, name="score")
             nc.scalar.activation(score[:], logit[:], SIGMOID, bias=fcb_sb[:])
-            nc.sync.dma_start(out[:, j * PIECE : (j + 1) * PIECE], score[:])
+            nc.sync.dma_start(out[:, u * UNIT : (u + 1) * UNIT], score[:])

@@ -7,7 +7,7 @@ N = 1024
 BANK = 512
 PIECE = BANK
 UNIT = 256
-WARM = 8
+WARM = 5
 LOADS = 4
 FLOPS = 2 * P * (HALVES * P) * N + 2 * (HALVES * P) * P * N
 

@@ -7,8 +7,8 @@ N = 1024
 BANK = 512
 PIECE = BANK
 UNIT = 256
-WARM = 5
-LOADS = 4
+WARM = 8
+LOADS = 2
 FLOPS = 2 * P * (HALVES * P) * N + 2 * (HALVES * P) * P * N
 
 BF16, F32, U16 = mybir.dt.bfloat16, mybir.dt.float32, mybir.dt.uint16
@@ -29,15 +29,15 @@ def tile_discriminator_kernel(tc, table, wv, bv, fc_w, fc_b, offs, out):
 
         wv_sb = held.tile([P, HALVES * P], BF16, name="wv_sb")
         nc.scalar.dma_start(wv_sb[:], wv)
-        bv_sb = [held.tile([P, 1], F32, name=f"bv_sb{h}") for h in range(HALVES)]
-        for h in range(HALVES):
-            nc.scalar.dma_start(bv_sb[h][:], bv[h * P : (h + 1) * P, :])
 
         words = held.tile([P, V], BF16, name="words")
         for q in range(LOADS):
             queue = nc.sync if q % 2 == 0 else nc.scalar
             queue.dma_start(words[:, q * (V // LOADS) : (q + 1) * (V // LOADS)], table[:, q * (V // LOADS) : (q + 1) * (V // LOADS)])
 
+        bv_sb = [held.tile([P, 1], F32, name=f"bv_sb{h}") for h in range(HALVES)]
+        for h in range(HALVES):
+            nc.scalar.dma_start(bv_sb[h][:], bv[h * P : (h + 1) * P, :])
         fcb_sb = held.tile([P, 1], F32, name="fcb_sb")
         nc.scalar.dma_start(fcb_sb[:], fc_b)
         fcw_sb = held.tile([P, HALVES, P], BF16, name="fcw_sb")

@@ -5,8 +5,8 @@ V = 4096
 HALVES = 2
 N = 1024
 BANK = 512
-PIECE = BANK
-UNIT = 256
+PIECE = 256
+BANKS = 8
 WARM = 8
 LOADS = 2
 FLOPS = 2 * P * (HALVES * P) * N + 2 * (HALVES * P) * P * N
@@ -20,9 +20,8 @@ def tile_discriminator_kernel(tc, table, wv, bv, fc_w, fc_b, offs, out):
     nc = tc.nc
     with (
         tc.tile_pool(name="held", bufs=1) as held,
-        tc.tile_pool(name="work", bufs=N // UNIT) as work,
-        tc.psum_pool(name="banks", bufs=1) as banks,
-        tc.psum_pool(name="logits", bufs=3) as logits,
+        tc.tile_pool(name="work", bufs=N // PIECE) as work,
+        tc.psum_pool(name="banks", bufs=BANKS) as banks,
     ):
         offsets = held.tile([P, N // 16], U16, name="offsets")
         nc.sync.dma_start(offsets[:], offs)
@@ -45,7 +44,7 @@ def tile_discriminator_kernel(tc, table, wv, bv, fc_w, fc_b, offs, out):
 
         idle = held.tile([P, BANK], BF16, name="idle")
         nc.vector.memset(idle[:], 0.0)
-        spin = banks.tile([P, BANK], F32, name="spin")
+        spin = banks.tile([P, BANK], F32, name="spin", tag="bank")
         for turn in range(WARM):
             nc.tensor.matmul(spin[:], idle[:, 0:P], idle[:], start=True, stop=True)
 
@@ -53,27 +52,25 @@ def tile_discriminator_kernel(tc, table, wv, bv, fc_w, fc_b, offs, out):
         nc.vector.memset(warm[:], 0.0)
         nc.scalar.activation(warm[:], warm[:], SIGMOID)
 
-        proj = [[banks.tile([P, PIECE], F32, name=f"proj{j}{h}") for h in range(HALVES)] for j in range(N // PIECE)]
+        proj = [[banks.tile([P, PIECE], F32, name=f"proj{j}{h}", tag="bank") for h in range(HALVES)] for j in range(N // PIECE)]
         for j in range(N // PIECE):
             piece = offsets[:, j * (PIECE // 16) : (j + 1) * (PIECE // 16)]
             for h in range(HALVES):
                 nc.tensor.matmul(proj[j][h][:], wv_sb[:, h * P : (h + 1) * P], words[:].indirect(piece), start=True, stop=True)
 
-        for u in range(N // UNIT):
-            j, col = divmod(u * UNIT, PIECE)
-
+        for j in range(N // PIECE):
             hidden = []
             for h in range(HALVES):
-                hid = work.tile([P, UNIT], BF16, name=f"hid{h}")
-                if j == 0 and h == 1:
-                    nc.scalar.activation(hid[:], proj[j][h][:, col : col + UNIT], RELU, bias=bv_sb[h][:])
+                hid = work.tile([P, PIECE], BF16, name=f"hid{h}")
+                if h == 1 and j < N // PIECE - 1:
+                    nc.scalar.activation(hid[:], proj[j][h][:], RELU, bias=bv_sb[h][:])
                 else:
-                    nc.vector.tensor_scalar(hid[:], proj[j][h][:, col : col + UNIT], bv_sb[h][:], 0.0, ADD, MAX)
+                    nc.vector.tensor_scalar(hid[:], proj[j][h][:], bv_sb[h][:], 0.0, ADD, MAX)
                 hidden.append(hid)
 
-            logit = logits.tile([P, UNIT], F32, name="logit")
+            logit = banks.tile([P, PIECE], F32, name="logit", tag="bank")
             for h in range(HALVES):
                 nc.tensor.matmul(logit[:], fcw_sb[:, h, :], hidden[h][:], start=(h == 0), stop=(h == HALVES - 1))
-            score = work.tile([P, UNIT], F32, name="score")
+            score = work.tile([P, PIECE], F32, name="score")
             nc.scalar.activation(score[:], logit[:], SIGMOID, bias=fcb_sb[:])
-            nc.sync.dma_start(out[:, u * UNIT : (u + 1) * UNIT], score[:])
+            nc.sync.dma_start(out[:, j * PIECE : (j + 1) * PIECE], score[:])

@@ -34,13 +34,12 @@ def tile_discriminator_kernel(tc, table, wv, bv, fc_w, fc_b, offs, out):
             queue = nc.sync if q % 2 == 0 else nc.scalar
             queue.dma_start(words[:, q * (V // LOADS) : (q + 1) * (V // LOADS)], table[:, q * (V // LOADS) : (q + 1) * (V // LOADS)])
 
-        bv_sb = [held.tile([P, 1], F32, name=f"bv_sb{h}") for h in range(HALVES)]
-        for h in range(HALVES):
-            nc.scalar.dma_start(bv_sb[h][:], bv[h * P : (h + 1) * P, :])
+        bv_sb = held.tile([P, HALVES], F32, name="bv_sb")
+        nc.gpsimd.dma_start(bv_sb[:], bv.rearrange("(h p) o -> p (h o)", p=P))
         fcb_sb = held.tile([P, 1], F32, name="fcb_sb")
-        nc.scalar.dma_start(fcb_sb[:], fc_b)
+        nc.gpsimd.dma_start(fcb_sb[:], fc_b)
         fcw_sb = held.tile([P, HALVES, P], BF16, name="fcw_sb")
-        nc.scalar.dma_start(fcw_sb[:], fc_w.rearrange("(h p) c -> p h c", p=P))
+        nc.gpsimd.dma_start(fcw_sb[:], fc_w.rearrange("(h p) c -> p h c", p=P))
 
         idle = held.tile([P, BANK], BF16, name="idle")
         nc.vector.memset(idle[:], 0.0)
@@ -63,9 +62,9 @@ def tile_discriminator_kernel(tc, table, wv, bv, fc_w, fc_b, offs, out):
             for h in range(HALVES):
                 hid = work.tile([P, PIECE], BF16, name=f"hid{h}")
                 if h == 1 and j < N // PIECE - 1:
-                    nc.scalar.activation(hid[:], proj[j][h][:], RELU, bias=bv_sb[h][:])
+                    nc.scalar.activation(hid[:], proj[j][h][:], RELU, bias=bv_sb[:, h : h + 1])
                 else:
-                    nc.vector.tensor_scalar(hid[:], proj[j][h][:], bv_sb[h][:], 0.0, ADD, MAX)
+                    nc.vector.tensor_scalar(hid[:], proj[j][h][:], bv_sb[:, h : h + 1], 0.0, ADD, MAX)
                 hidden.append(hid)
 
             logit = banks.tile([P, PIECE], F32, name="logit", tag="bank")

@@ -26,8 +26,10 @@ def tile_discriminator_kernel(tc, table, wv, bv, fc_w, fc_b, offs, out):
         offsets = held.tile([P, N // 16], U16, name="offsets")
         nc.sync.dma_start(offsets[:], offs)
 
-        wv_sb = held.tile([P, HALVES * P], BF16, name="wv_sb")
-        nc.scalar.dma_start(wv_sb[:], wv)
+        wv_in = held.tile([P, P, HALVES], BF16, name="wv_in")
+        nc.scalar.dma_start(wv_in[:], wv.rearrange("d (p h) -> d p h", h=HALVES))
+        wv_sb = held.tile([P, HALVES, P], BF16, name="wv_sb")
+        nc.vector.tensor_copy(wv_sb[:], wv_in[:].rearrange("d p h -> d h p"))
 
         words = held.tile([P, V], BF16, name="words")
         for q in range(LOADS):
@@ -35,11 +37,11 @@ def tile_discriminator_kernel(tc, table, wv, bv, fc_w, fc_b, offs, out):
             queue.dma_start(words[:, q * (V // LOADS) : (q + 1) * (V // LOADS)], table[:, q * (V // LOADS) : (q + 1) * (V // LOADS)])
 
         bv_sb = held.tile([P, HALVES], F32, name="bv_sb")
-        nc.gpsimd.dma_start(bv_sb[:], bv.rearrange("(h p) o -> p (h o)", p=P))
+        nc.gpsimd.dma_start(bv_sb[:], bv.rearrange("(p h) o -> p (h o)", h=HALVES))
         fcb_sb = held.tile([P, 1], F32, name="fcb_sb")
         nc.gpsimd.dma_start(fcb_sb[:], fc_b)
         fcw_sb = held.tile([P, HALVES, P], BF16, name="fcw_sb")
-        nc.gpsimd.dma_start(fcw_sb[:], fc_w.rearrange("(h p) c -> p h c", p=P))
+        nc.gpsimd.dma_start(fcw_sb[:], fc_w.rearrange("(p h) c -> p h c", h=HALVES))
 
         idle = held.tile([P, BANK], BF16, name="idle")
         nc.vector.memset(idle[:], 0.0)
@@ -55,7 +57,7 @@ def tile_discriminator_kernel(tc, table, wv, bv, fc_w, fc_b, offs, out):
         for j in range(N // PIECE):
             piece = offsets[:, j * (PIECE // 16) : (j + 1) * (PIECE // 16)]
             for h in range(HALVES):
-                nc.tensor.matmul(proj[j][h][:], wv_sb[:, h * P : (h + 1) * P], words[:].indirect(piece), start=True, stop=True)
+                nc.tensor.matmul(proj[j][h][:], wv_sb[:, h, :], words[:].indirect(piece), start=True, stop=True)
 
         for j in range(N // PIECE):
             hidden = []

@@ -8,6 +8,7 @@ BANK = 512
 PIECE = 256
 BANKS = 8
 WARM = 8
+SQUARE = 32
 LOADS = 2
 FLOPS = 2 * P * (HALVES * P) * N + 2 * (HALVES * P) * P * N
 
@@ -29,17 +30,18 @@ def tile_discriminator_kernel(tc, table, wv, bv, fc_w, fc_b, offs, out):
         wv_in = held.tile([P, P, HALVES], BF16, name="wv_in")
         nc.scalar.dma_start(wv_in[:], wv.rearrange("d (p h) -> d p h", h=HALVES))
         wv_sb = held.tile([P, HALVES, P], BF16, name="wv_sb")
-        nc.vector.tensor_copy(wv_sb[:], wv_in[:].rearrange("d p h -> d h p"))
 
         words = held.tile([P, V], BF16, name="words")
         for q in range(LOADS):
             queue = nc.sync if q % 2 == 0 else nc.scalar
             queue.dma_start(words[:, q * (V // LOADS) : (q + 1) * (V // LOADS)], table[:, q * (V // LOADS) : (q + 1) * (V // LOADS)])
 
-        bv_sb = held.tile([P, HALVES], F32, name="bv_sb")
-        nc.gpsimd.dma_start(bv_sb[:], bv.rearrange("(p h) o -> p (h o)", h=HALVES))
-        fcb_sb = held.tile([P, 1], F32, name="fcb_sb")
-        nc.gpsimd.dma_start(fcb_sb[:], fc_b)
+        bv_rows = held.tile([P, SQUARE, HALVES], F32, name="bv_rows")
+        nc.vector.memset(bv_rows[:], 0.0)
+        nc.gpsimd.dma_start(bv_rows[0:P:SQUARE, :, :], bv.rearrange("(g c h) o -> g c (h o)", c=SQUARE, h=HALVES))
+        bias_rows = held.tile([P, 4, SQUARE], F32, name="bias_rows", align_bytes=64)
+        nc.vector.memset(bias_rows[:], 0.0)
+        nc.gpsimd.dma_start(bias_rows[0:P:SQUARE, HALVES, :], fc_b.rearrange("(g c) o -> g (c o)", c=SQUARE))
         fcw_sb = held.tile([P, HALVES, P], BF16, name="fcw_sb")
         nc.gpsimd.dma_start(fcw_sb[:], fc_w.rearrange("(p h) c -> p h c", h=HALVES))
 
@@ -53,6 +55,13 @@ def tile_discriminator_kernel(tc, table, wv, bv, fc_w, fc_b, offs, out):
         nc.vector.memset(warm[:], 0.0)
         nc.scalar.activation(warm[:], warm[:], SIGMOID)
 
+        nc.vector.tensor_copy(wv_sb[:], wv_in[:].rearrange("d p h -> d h p"))
+        nc.vector.tensor_copy(bias_rows[:, 0:HALVES, :], bv_rows[:].rearrange("r c h -> r h c"))
+        biases = held.tile([P, 4, SQUARE], F32, name="biases", align_bytes=64)
+        nc.vector.transpose(biases[:], bias_rows[:])
+        bv_sb = [biases[:, h, 0:1] for h in range(HALVES)]
+        fcb_sb = biases[:, HALVES, 0:1]
+
         proj = [[banks.tile([P, PIECE], F32, name=f"proj{j}{h}", tag="bank") for h in range(HALVES)] for j in range(N // PIECE)]
         for j in range(N // PIECE):
             piece = offsets[:, j * (PIECE // 16) : (j + 1) * (PIECE // 16)]
@@ -64,14 +73,14 @@ def tile_discriminator_kernel(tc, table, wv, bv, fc_w, fc_b, offs, out):
             for h in range(HALVES):
                 hid = work.tile([P, PIECE], BF16, name=f"hid{h}")
                 if h == 1 and j < N // PIECE - 1:
-                    nc.scalar.activation(hid[:], proj[j][h][:], RELU, bias=bv_sb[:, h : h + 1])
+                    nc.scalar.activation(hid[:], proj[j][h][:], RELU, bias=bv_sb[h])
                 else:
-                    nc.vector.tensor_scalar(hid[:], proj[j][h][:], bv_sb[:, h : h + 1], 0.0, ADD, MAX)
+                    nc.vector.tensor_scalar(hid[:], proj[j][h][:], bv_sb[h], 0.0, ADD, MAX)
                 hidden.append(hid)
 
             logit = banks.tile([P, PIECE], F32, name="logit", tag="bank")
             for h in range(HALVES):
                 nc.tensor.matmul(logit[:], fcw_sb[:, h, :], hidden[h][:], start=(h == 0), stop=(h == HALVES - 1))
             score = work.tile([P, PIECE], F32, name="score")
-            nc.scalar.activation(score[:], logit[:], SIGMOID, bias=fcb_sb[:])
+            nc.scalar.activation(score[:], logit[:], SIGMOID, bias=fcb_sb)
             nc.sync.dma_start(out[:, j * PIECE : (j + 1) * PIECE], score[:])

@@ -5,7 +5,8 @@ V = 4096
 HALVES = 2
 N = 1024
 BANK = 512
-PIECE = 256
+PIECES = (192, 256, 288, 288)
+STARTS = tuple(sum(PIECES[:j]) for j in range(len(PIECES)))
 BANKS = 8
 WARM = 8
 SQUARE = 32
@@ -21,7 +22,7 @@ def tile_discriminator_kernel(tc, table, wv, bv, fc_w, fc_b, offs, out):
     nc = tc.nc
     with (
         tc.tile_pool(name="held", bufs=1) as held,
-        tc.tile_pool(name="work", bufs=N // PIECE) as work,
+        tc.tile_pool(name="work", bufs=len(PIECES)) as work,
         tc.psum_pool(name="banks", bufs=BANKS) as banks,
     ):
         offsets = held.tile([P, N // 16], U16, name="offsets")
@@ -62,25 +63,25 @@ def tile_discriminator_kernel(tc, table, wv, bv, fc_w, fc_b, offs, out):
         bv_sb = [biases[:, h, 0:1] for h in range(HALVES)]
         fcb_sb = biases[:, HALVES, 0:1]
 
-        proj = [[banks.tile([P, PIECE], F32, name=f"proj{j}{h}", tag="bank") for h in range(HALVES)] for j in range(N // PIECE)]
-        for j in range(N // PIECE):
-            piece = offsets[:, j * (PIECE // 16) : (j + 1) * (PIECE // 16)]
+        proj = [[banks.tile([P, n], F32, name=f"proj{j}{h}", tag="bank") for h in range(HALVES)] for j, n in enumerate(PIECES)]
+        for j, (start, n) in enumerate(zip(STARTS, PIECES)):
+            piece = offsets[:, start // 16 : (start + n) // 16]
             for h in range(HALVES):
                 nc.tensor.matmul(proj[j][h][:], wv_sb[:, h, :], words[:].indirect(piece), start=True, stop=True)
 
-        for j in range(N // PIECE):
+        for j, (start, n) in enumerate(zip(STARTS, PIECES)):
             hidden = []
             for h in range(HALVES):
-                hid = work.tile([P, PIECE], BF16, name=f"hid{h}")
-                if h == 1 and j < N // PIECE - 1:
+                hid = work.tile([P, n], BF16, name=f"hid{h}")
+                if h == 1 and j < len(PIECES) - 1:
                     nc.scalar.activation(hid[:], proj[j][h][:], RELU, bias=bv_sb[h])
                 else:
                     nc.vector.tensor_scalar(hid[:], proj[j][h][:], bv_sb[h], 0.0, ADD, MAX)
                 hidden.append(hid)
 
-            logit = banks.tile([P, PIECE], F32, name="logit", tag="bank")
+            logit = banks.tile([P, n], F32, name="logit", tag="bank")
             for h in range(HALVES):
                 nc.tensor.matmul(logit[:], fcw_sb[:, h, :], hidden[h][:], start=(h == 0), stop=(h == HALVES - 1))
-            score = work.tile([P, PIECE], F32, name="score")
+            score = work.tile([P, n], F32, name="score")
             nc.scalar.activation(score[:], logit[:], SIGMOID, bias=fcb_sb)
-            nc.sync.dma_start(out[:, j * PIECE : (j + 1) * PIECE], score[:])
+            nc.sync.dma_start(out[:, start : start + n], score[:])

import concourse.mybir as mybir

P = 128
V = 4096
HALVES = 2
N = 1024
BANK = 512
PIECES = (192, 256, 288, 288)
STARTS = tuple(sum(PIECES[:j]) for j in range(len(PIECES)))
BANKS = 8
WARM = 8
SQUARE = 32
LOADS = 2
FLOPS = 2 * P * (HALVES * P) * N + 2 * (HALVES * P) * P * N

BF16, F32, U16 = mybir.dt.bfloat16, mybir.dt.float32, mybir.dt.uint16
ADD, MAX = mybir.AluOpType.add, mybir.AluOpType.max
RELU, SIGMOID = mybir.ActivationFunctionType.Relu, mybir.ActivationFunctionType.Sigmoid


def tile_discriminator_kernel(tc, table, wv, bv, fc_w, fc_b, offs, out):
    nc = tc.nc
    with (
        tc.tile_pool(name="held", bufs=1) as held,
        tc.tile_pool(name="work", bufs=len(PIECES)) as work,
        tc.psum_pool(name="banks", bufs=BANKS) as banks,
    ):
        offsets = held.tile([P, N // 16], U16, name="offsets")
        nc.sync.dma_start(offsets[:], offs)

        wv_in = held.tile([P, P, HALVES], BF16, name="wv_in")
        nc.scalar.dma_start(wv_in[:], wv.rearrange("d (p h) -> d p h", h=HALVES))
        wv_sb = held.tile([P, HALVES, P], BF16, name="wv_sb")

        words = held.tile([P, V], BF16, name="words")
        for q in range(LOADS):
            queue = nc.sync if q % 2 == 0 else nc.scalar
            queue.dma_start(words[:, q * (V // LOADS) : (q + 1) * (V // LOADS)], table[:, q * (V // LOADS) : (q + 1) * (V // LOADS)])

        bv_rows = held.tile([P, SQUARE, HALVES], F32, name="bv_rows")
        nc.vector.memset(bv_rows[:], 0.0)
        nc.gpsimd.dma_start(bv_rows[0:P:SQUARE, :, :], bv.rearrange("(g c h) o -> g c (h o)", c=SQUARE, h=HALVES))
        bias_rows = held.tile([P, 4, SQUARE], F32, name="bias_rows", align_bytes=64)
        nc.vector.memset(bias_rows[:], 0.0)
        nc.gpsimd.dma_start(bias_rows[0:P:SQUARE, HALVES, :], fc_b.rearrange("(g c) o -> g (c o)", c=SQUARE))
        fcw_sb = held.tile([P, HALVES, P], BF16, name="fcw_sb")
        nc.gpsimd.dma_start(fcw_sb[:], fc_w.rearrange("(p h) c -> p h c", h=HALVES))

        idle = held.tile([P, BANK], BF16, name="idle")
        nc.vector.memset(idle[:], 0.0)
        spin = banks.tile([P, BANK], F32, name="spin", tag="bank")
        for turn in range(WARM):
            nc.tensor.matmul(spin[:], idle[:, 0:P], idle[:], start=True, stop=True)

        warm = held.tile([P, 1], F32, name="warm")
        nc.vector.memset(warm[:], 0.0)
        nc.scalar.activation(warm[:], warm[:], SIGMOID)

        nc.vector.tensor_copy(wv_sb[:], wv_in[:].rearrange("d p h -> d h p"))
        nc.vector.tensor_copy(bias_rows[:, 0:HALVES, :], bv_rows[:].rearrange("r c h -> r h c"))
        biases = held.tile([P, 4, SQUARE], F32, name="biases", align_bytes=64)
        nc.vector.transpose(biases[:], bias_rows[:])
        bv_sb = [biases[:, h, 0:1] for h in range(HALVES)]
        fcb_sb = biases[:, HALVES, 0:1]

        proj = [[banks.tile([P, n], F32, name=f"proj{j}{h}", tag="bank") for h in range(HALVES)] for j, n in enumerate(PIECES)]
        for j, (start, n) in enumerate(zip(STARTS, PIECES)):
            piece = offsets[:, start // 16 : (start + n) // 16]
            for h in range(HALVES):
                nc.tensor.matmul(proj[j][h][:], wv_sb[:, h, :], words[:].indirect(piece), start=True, stop=True)

        for j, (start, n) in enumerate(zip(STARTS, PIECES)):
            hidden = []
            for h in range(HALVES):
                hid = work.tile([P, n], BF16, name=f"hid{h}")
                if h == 1 and j < len(PIECES) - 1:
                    nc.scalar.activation(hid[:], proj[j][h][:], RELU, bias=bv_sb[h])
                else:
                    nc.vector.tensor_scalar(hid[:], proj[j][h][:], bv_sb[h], 0.0, ADD, MAX)
                hidden.append(hid)

            logit = banks.tile([P, n], F32, name="logit", tag="bank")
            for h in range(HALVES):
                nc.tensor.matmul(logit[:], fcw_sb[:, h, :], hidden[h][:], start=(h == 0), stop=(h == HALVES - 1))
            score = work.tile([P, n], F32, name="score")
            nc.scalar.activation(score[:], logit[:], SIGMOID, bias=fcb_sb)
            nc.sync.dma_start(out[:, start : start + n], score[:])
